import numpy as np
import ml_dtypes


def mxq(x, axis, fmt="e4m3"):
    dtype, down = {"e4m3": (ml_dtypes.float8_e4m3fn, 7), "e5m2": (ml_dtypes.float8_e5m2, 14)}[fmt]
    v = np.moveaxis(np.asarray(x, np.float32).astype(ml_dtypes.bfloat16).astype(np.float64), axis, -1)
    blocks = v.reshape(v.shape[:-1] + (-1, 32))
    amax = np.abs(blocks).max(-1, keepdims=True)
    byte = np.maximum(np.where(amax > 0, np.frexp(amax)[1] - 1 + 127, 0) - down, 1)
    scale = np.exp2(byte - 127.0)
    codes = (blocks / scale).astype(np.float32).astype(dtype).astype(np.float64)
    return np.moveaxis((codes * scale).reshape(v.shape), -1, axis)


WIDE = False


def mx_kscale(k):
    if not WIDE:
        return np.ones(k)
    levels = np.array([10, -10, 5, -5, 0])
    a = np.random.permutation(np.resize(levels, k // 512 * 4)).reshape(k // 512, 4)
    idx = np.arange(k)
    return np.exp2(a[idx // 512, idx % 128 // 32])


BF16 = ml_dtypes.bfloat16


def bf(x):
    return np.asarray(x, np.float32).astype(BF16)


def f64(x):
    return np.asarray(x).astype(np.float64)


B, T, I, H = 128, 8, 1024, 1024


def sigmoid(v):
    return 1.0 / (1.0 + np.exp(-v))


def setup_inputs():
    s = mx_kscale(I)
    d = {"inputs": bf(np.random.standard_normal((B, T, I)) * s),
         "h0": bf(np.random.standard_normal((1, B, H))),
         "c0": bf(np.random.standard_normal((1, B, H)))}
    for ni, nh in (("ii", "hi"), ("if_", "hf"), ("io", "ho"), ("ig", "hg")):
        d["w_" + ni] = bf(np.random.standard_normal((H, I)) / np.sqrt(I) / s[None, :])
        d["b_" + ni] = bf(np.random.standard_normal((H, 1)) * 0.3)
        d["w_" + nh] = bf(np.random.standard_normal((H, H)) * 0.7 / np.sqrt(H))
        d["b_" + nh] = bf(np.random.standard_normal((H, 1)) * 0.3)
    return d


def reference(inputs, h0, c0, w_ii, b_ii, w_hi, b_hi, w_if_, b_if_, w_hf, b_hf, w_io, b_io, w_ho, b_ho, w_ig, b_ig, w_hg, b_hg):
    xq = mxq(f64(inputs), 2, "e4m3")
    h0s = f64(h0)[0]
    c0s = f64(c0)[0]
    zi = (xq @ mxq(f64(w_ii), 1, "e4m3").T) + (h0s @ f64(w_hi).T)[:, None, :] + f64(b_ii)[:, 0] + f64(b_hi)[:, 0]
    zf = (xq @ mxq(f64(w_if_), 1, "e4m3").T) + (h0s @ f64(w_hf).T)[:, None, :] + f64(b_if_)[:, 0] + f64(b_hf)[:, 0]
    zg = (xq @ mxq(f64(w_ig), 1, "e4m3").T) + (h0s @ f64(w_hg).T)[:, None, :] + f64(b_ig)[:, 0] + f64(b_hg)[:, 0]
    zo = (xq @ mxq(f64(w_io), 1, "e4m3").T) + (h0s @ f64(w_ho).T)[:, None, :] + f64(b_io)[:, 0] + f64(b_ho)[:, 0]
    i = sigmoid(zi)
    f = sigmoid(zf)
    g = np.tanh(zg)
    o = sigmoid(zo)
    c_next = f * c0s[:, None, :] + i * g
    h_next = o * np.tanh(c_next)
    hidden_seq = np.transpose(h_next, (1, 0, 2))
    h_last = hidden_seq[-1][None]
    c_last = c_next[:, -1][None]
    return hidden_seq, h_last, c_last

@@ -1,0 +1,273 @@
+from contextlib import ExitStack
+
+import concourse.mybir as mybir
+from concourse.masks import make_identity
+
+F32 = mybir.dt.float32
+BF16 = mybir.dt.bfloat16
+U32 = mybir.dt.uint32
+U8 = mybir.dt.uint8
+I32 = mybir.dt.int32
+FP8X4 = mybir.dt.float8_e4m3fn_x4
+ACT = mybir.ActivationFunctionType
+ALU = mybir.AluOpType
+
+P = 128
+B, T, I, H = 128, 8, 1024, 1024
+NG = 4
+NCH = H // P
+NT = 4
+RAW_BUFS = 24
+PINNED = False
+
+FLOPS = 2 * B * T * I * NG * H + 2 * B * H * NG * H
+
+
+def tile_naivelstm_pa_kernel(
+    tc,
+    inputs, h0, c0,
+    w_ii, b_ii, w_hi, b_hi,
+    w_if_, b_if_, w_hf, b_hf,
+    w_io, b_io, w_ho, b_ho,
+    w_ig, b_ig, w_hg, b_hg,
+    out_0, out_1, out_2,
+):
+    nc = tc.nc
+    w_in = [w_ii, w_if_, w_io, w_ig]
+    w_hid = [w_hi, w_hf, w_ho, w_hg]
+    b_in = [b_ii, b_if_, b_io, b_ig]
+    b_hid = [b_hi, b_hf, b_ho, b_hg]
+
+    with ExitStack() as ctx:
+        if PINNED:
+            ctx.enter_context(tc.manual_schedule())
+        const = ctx.enter_context(tc.tile_pool(name="const", bufs=1))
+        raw = ctx.enter_context(tc.tile_pool(name="raw", bufs=RAW_BUFS))
+        wgp = ctx.enter_context(tc.tile_pool(name="wgp", bufs=2))
+        wqp = ctx.enter_context(tc.tile_pool(name="wqp", bufs=3))
+        whp = ctx.enter_context(tc.tile_pool(name="whp", bufs=2))
+        zp = ctx.enter_context(tc.tile_pool(name="zp", bufs=4))
+        hp = ctx.enter_context(tc.tile_pool(name="hp", bufs=3))
+        psum = ctx.enter_context(tc.psum_pool(name="psum", bufs=8))
+
+        ident = const.tile([P, P], F32, name="ident")
+        ones = const.tile([P, P], BF16, name="ones")
+        scratch = const.tile([P, 1], F32, name="scratch")
+        bias_sb = const.tile([P, NCH, NG, P], BF16, name="bias_sb")
+        h0_raw = const.tile([P, H], BF16, name="h0_raw")
+        c0_sb = const.tile([P, H], BF16, name="c0_sb")
+        h_t = const.tile([P, 4, 2, P], BF16, name="h_t")
+        x_raw = const.tile([P, T, I], BF16, name="x_raw")
+        xg = const.tile([P, T, I], BF16, name="xg", align_bytes=64)
+        xq = const.tile([P, T, I // 4], U32, name="xq", align_bytes=64)
+        xs = const.tile([P, T, I // 4], U8, name="xs", align_bytes=64)
+        gsum = const.tile([P, NCH, NG * P], F32, name="gsum")
+
+        make_identity(nc, ident[:])
+        nc.vector.memset(scratch[:], 0.0)
+        nc.scalar.activation(out=scratch[:], in_=scratch[:], func=ACT.Sigmoid)
+        nc.vector.memset(ones[:], 1.0)
+        nc.vector.memset(bias_sb[:].bitcast(I32), 0)
+
+        blocks = []
+        for k in (0, 1):
+            blocks.extend([(1, k, g) for g in range(NG)])
+        blocks.extend([(0, 0, g) for g in range(NG)])
+        for k in range(NCH):
+            if k + 2 < NCH:
+                blocks.extend([(1, k + 2, g) for g in range(NG)])
+            if k + 1 < NCH:
+                blocks.extend([(0, k + 1, g) for g in range(NG)])
+        raw_tiles = {}
+        cursor = [0]
+
+        def issue_load():
+            n = cursor[0]
+            if n < len(blocks):
+                hid, k, g = blocks[n]
+                w = w_hid[g] if hid else w_in[g]
+                wraw = raw.tile([P, I], BF16, name="wraw", tag="wraw")
+                nc.sync.dma_start(out=wraw[:], in_=w[k * P:(k + 1) * P, :])
+                raw_tiles[blocks[n]] = wraw
+                cursor[0] = n + 1
+
+        def load_x(pair):
+            nc.sync.dma_start(
+                out=x_raw[:, 2 * pair:2 * pair + 2, :],
+                in_=inputs[:, 2 * pair:2 * pair + 2, :],
+            )
+
+        nc.sync.dma_start(out=h0_raw[:], in_=h0[0])
+        for n in range(4):
+            issue_load()
+        load_x(0)
+        load_x(1)
+        for n in range(4):
+            issue_load()
+        load_x(2)
+        load_x(3)
+        for n in range(RAW_BUFS - 8):
+            issue_load()
+        for g in range(NG):
+            nc.scalar.dma_start(
+                out=bias_sb[0:1, :, g, :],
+                in_=b_in[g].rearrange("(k r) o -> o k r", r=P),
+            )
+            nc.scalar.dma_start(
+                out=bias_sb[1:2, :, g, :],
+                in_=b_hid[g].rearrange("(k r) o -> o k r", r=P),
+            )
+        nc.scalar.dma_start(out=c0_sb[:], in_=c0[0])
+
+        def copy(engine, out, in_):
+            if engine == 0:
+                nc.vector.tensor_copy(out=out, in_=in_)
+            else:
+                nc.scalar.copy(out=out, in_=in_)
+
+        def transpose_words(words):
+            bank = psum.tile([P, 4, P], F32, name="tp", tag="bank")
+            for q in range(4):
+                nc.tensor.transpose(bank[:, q, :], words[:, q * P:(q + 1) * P], ident[:])
+            return bank
+
+        def regrouped(bank):
+            return bank[:].rearrange("p (g u) r -> p g r u", u=2)
+
+        def prep_h0():
+            bank = transpose_words(h0_raw[:].bitcast(F32))
+            nc.vector.tensor_copy(
+                out=h_t[:],
+                in_=bank[:].bitcast(BF16).rearrange("p j (b e) -> p j e b", e=2),
+            )
+
+        def prep_x(pair):
+            for t in (2 * pair, 2 * pair + 1):
+                bank = transpose_words(x_raw[:].bitcast(F32)[:, t, :])
+                copy(
+                    t % 2,
+                    xg[:].bitcast(F32)[:, t, :].rearrange("p (g r u) -> p g r u", g=2, u=2),
+                    regrouped(bank),
+                )
+            tt = slice(2 * pair, 2 * pair + 2)
+            nc.vector.quantize_mx(
+                out=xq[:, tt, :].rearrange("p t c -> p (t c)").bitcast(FP8X4),
+                scales=xs[:, tt, :].rearrange("p t c -> p (t c)"),
+                in_=xg[:, tt, :].rearrange("p t c -> p (t c)"),
+            )
+
+        wh_tiles = {}
+        wq_tiles = {}
+
+        def prep_hidden_weights(k):
+            wh_t = whp.tile([P, 4, NG * P], F32, name="wh_t")
+            wh_tiles[k] = wh_t
+            for g in range(NG):
+                bank = transpose_words(raw_tiles[(1, k, g)][:].bitcast(F32))
+                copy(1, wh_t[:, :, g * P:(g + 1) * P], bank[:])
+                issue_load()
+
+        def hidden(k):
+            wv = wh_tiles[k][:].bitcast(BF16).rearrange("p j (c e) -> p j c e", e=2)
+            bank = psum.tile([P, NG * P], F32, name="hid", tag="bank")
+            for j in range(4):
+                for e in range(2):
+                    nc.tensor.matmul(
+                        bank[:], lhsT=h_t[:, j, e, :], rhs=wv[:, j, :, e],
+                        start=(j == 0 and e == 0), stop=False,
+                    )
+            nc.tensor.matmul(
+                bank[:], lhsT=ones[:],
+                rhs=bias_sb[:, k, :, :].rearrange("p g r -> p (g r)"),
+                start=False, stop=True,
+            )
+            copy(1, gsum[:, k, :], bank[:])
+
+        def prep_input_weights(k):
+            wg = wgp.tile([P, 2, NG, 4 * P], BF16, name="wg", align_bytes=64)
+            wq = wqp.tile([P, 2, NG * P], U32, name="wq", align_bytes=64)
+            ws = wqp.tile([P, 2, NG * P], U8, name="ws", align_bytes=64)
+            wq_tiles[k] = (wq, ws)
+            for g in range(NG):
+                bank = transpose_words(raw_tiles[(0, k, g)][:].bitcast(F32))
+                copy(
+                    0 if g < 2 else 1,
+                    wg[:].bitcast(F32)[:, :, g, :].rearrange("p g (r u) -> p g r u", u=2),
+                    regrouped(bank),
+                )
+                issue_load()
+            nc.vector.quantize_mx(
+                out=wq[:].rearrange("p g c -> p (g c)").bitcast(FP8X4),
+                scales=ws[:].rearrange("p g c -> p (g c)"),
+                in_=wg[:].rearrange("p g n c -> p (g n c)"),
+            )
+
+        def gates(k, tg):
+            wq, ws = wq_tiles[k]
+            z = zp.tile([P, NG, NT, P], F32, name="z")
+            for tl in range(NT):
+                t = tg * NT + tl
+                bank = psum.tile([P, NG, P], F32, name="mx", tag="bank")
+                for g in range(2):
+                    cols = slice(g * P, (g + 1) * P)
+                    nc.tensor.matmul_mx(
+                        out=bank[:].rearrange("p g r -> p (g r)"),
+                        lhsT=xq[:, t, cols].bitcast(FP8X4),
+                        lhsT_scale=xs[:, t, cols],
+                        rhs=wq[:, g, :].bitcast(FP8X4),
+                        rhs_scale=ws[:, g, :],
+                        start=(g == 0),
+                        stop=(g == 1),
+                    )
+                nc.vector.tensor_tensor(
+                    out=z[:, :, tl, :],
+                    in0=bank[:],
+                    in1=gsum[:, k, :].rearrange("p (g r) -> p g r", g=NG),
+                    op=ALU.add,
+                )
+            return z
+
+        def elementwise(k, tg, z):
+            ks = slice(k * P, (k + 1) * P)
+            sig = z[:, 0:3, :, :].rearrange("p g t r -> p (g t r)")
+            nc.scalar.activation(out=sig, in_=sig, func=ACT.Sigmoid)
+            nc.scalar.activation(out=z[:, 3], in_=z[:, 3], func=ACT.Tanh)
+            nc.gpsimd.tensor_tensor(
+                out=z[:, 1], in0=z[:, 1],
+                in1=c0_sb[:, ks].unsqueeze(1).to_broadcast([P, NT, P]),
+                op=ALU.mult,
+            )
+            nc.gpsimd.tensor_tensor(out=z[:, 0], in0=z[:, 0], in1=z[:, 3], op=ALU.mult)
+            nc.vector.tensor_tensor(out=z[:, 3], in0=z[:, 0], in1=z[:, 1], op=ALU.add)
+            nc.scalar.activation(out=z[:, 1], in_=z[:, 3], func=ACT.Tanh)
+            hout = hp.tile([P, NT, P], F32, name="hout")
+            nc.vector.tensor_tensor(out=hout[:], in0=z[:, 2], in1=z[:, 1], op=ALU.mult)
+            t0 = tg * NT
+            nc.sync.dma_start(
+                out=out_0[t0:t0 + NT, :, ks].rearrange("t b h -> b t h"), in_=hout[:]
+            )
+            if t0 + NT == T:
+                nc.sync.dma_start(out=out_1[0, :, ks], in_=hout[:, NT - 1, :])
+                nc.sync.dma_start(out=out_2[0, :, ks], in_=z[:, 3, NT - 1, :])
+
+        prep_h0()
+        prep_hidden_weights(0)
+        hidden(0)
+        prep_x(0)
+        prep_x(1)
+        prep_hidden_weights(1)
+        hidden(1)
+        prep_x(2)
+        prep_x(3)
+        prep_input_weights(0)
+        for k in range(NCH):
+            if k + 2 < NCH:
+                prep_hidden_weights(k + 2)
+            z = gates(k, 0)
+            elementwise(k, 0, z)
+            if k + 1 < NCH:
+                prep_input_weights(k + 1)
+            if k + 2 < NCH:
+                hidden(k + 2)
+            z = gates(k, 1)
+            elementwise(k, 1, z)

@@ -18,7 +18,13 @@ NG = 4
 NCH = H // P
 NT = 4
 RAW_BUFS = 24
-PINNED = False
+PINNED = True
+NU = 2 * NCH
+TAIL_V = 3
+COPY_X = (0, 1)
+COPY_I = (0, 0, 0, 1)
+COPY_H = (1, 1, 1, 1)
+COPY_G = 1
 
 FLOPS = 2 * B * T * I * NG * H + 2 * B * H * NG * H
 
@@ -69,45 +75,46 @@ def tile_naivelstm_pa_kernel(
         nc.vector.memset(ones[:], 1.0)
         nc.vector.memset(bias_sb[:].bitcast(I32), 0)
 
+        plan = [("x", 0), ("x", 1), ("I", 0), ("h0", 0), ("H", 0), ("hid", 0)]
+        for u in range(NU):
+            k, half = divmod(u, 2)
+            plan.append(("U", u))
+            if u == 0:
+                plan.extend([("x", 2), ("x", 3), ("H", 1)])
+            elif u == 1:
+                plan.extend([("I", 1), ("hid", 1), ("H", 2)])
+            elif half == 0 and k + 1 < NCH:
+                plan.extend([("I", k + 1), ("hid", k + 1)])
+            elif half == 1 and k + 2 < NCH:
+                plan.append(("H", k + 2))
+
         blocks = []
-        for k in (0, 1):
-            blocks.extend([(1, k, g) for g in range(NG)])
-        blocks.extend([(0, 0, g) for g in range(NG)])
-        for k in range(NCH):
-            if k + 2 < NCH:
-                blocks.extend([(1, k + 2, g) for g in range(NG)])
-            if k + 1 < NCH:
-                blocks.extend([(0, k + 1, g) for g in range(NG)])
+        for kind, k in plan:
+            if kind == "H" or kind == "I":
+                blocks.extend([(kind, k, g) for g in range(NG)])
         raw_tiles = {}
         cursor = [0]
 
         def issue_load():
             n = cursor[0]
             if n < len(blocks):
-                hid, k, g = blocks[n]
-                w = w_hid[g] if hid else w_in[g]
+                kind, k, g = blocks[n]
+                w = w_hid[g] if kind == "H" else w_in[g]
                 wraw = raw.tile([P, I], BF16, name="wraw", tag="wraw")
                 nc.sync.dma_start(out=wraw[:], in_=w[k * P:(k + 1) * P, :])
                 raw_tiles[blocks[n]] = wraw
                 cursor[0] = n + 1
 
-        def load_x(pair):
-            nc.sync.dma_start(
-                out=x_raw[:, 2 * pair:2 * pair + 2, :],
-                in_=inputs[:, 2 * pair:2 * pair + 2, :],
-            )
-
-        nc.sync.dma_start(out=h0_raw[:], in_=h0[0])
-        for n in range(4):
-            issue_load()
-        load_x(0)
-        load_x(1)
-        for n in range(4):
-            issue_load()
-        load_x(2)
-        load_x(3)
-        for n in range(RAW_BUFS - 8):
-            issue_load()
+        for kind, k in plan:
+            if kind == "h0":
+                nc.sync.dma_start(out=h0_raw[:], in_=h0[0])
+            elif kind == "x":
+                nc.sync.dma_start(
+                    out=x_raw[:, 2 * k:2 * k + 2, :], in_=inputs[:, 2 * k:2 * k + 2, :]
+                )
+            elif (kind == "H" or kind == "I") and cursor[0] < RAW_BUFS:
+                for g in range(NG):
+                    issue_load()
         for g in range(NG):
             nc.scalar.dma_start(
                 out=bias_sb[0:1, :, g, :],
@@ -134,21 +141,25 @@ def tile_naivelstm_pa_kernel(
         def regrouped(bank):
             return bank[:].rearrange("p (g u) r -> p g r u", u=2)
 
-        def prep_h0():
-            bank = transpose_words(h0_raw[:].bitcast(F32))
-            nc.vector.tensor_copy(
-                out=h_t[:],
-                in_=bank[:].bitcast(BF16).rearrange("p j (b e) -> p j e b", e=2),
-            )
+        wh_tiles = {}
+        wg_tiles = {}
+        wq_tiles = {}
+        z_tiles = {}
+        state = {"late": None, "pending": []}
 
-        def prep_x(pair):
-            for t in (2 * pair, 2 * pair + 1):
-                bank = transpose_words(x_raw[:].bitcast(F32)[:, t, :])
-                copy(
-                    t % 2,
-                    xg[:].bitcast(F32)[:, t, :].rearrange("p (g r u) -> p g r u", g=2, u=2),
-                    regrouped(bank),
-                )
+        def flush_pending():
+            todo = state["pending"]
+            state["pending"] = []
+            for f in todo:
+                f()
+
+        def run_late():
+            f = state["late"]
+            state["late"] = None
+            if f is not None:
+                f()
+
+        def quantise_x(pair):
             tt = slice(2 * pair, 2 * pair + 2)
             nc.vector.quantize_mx(
                 out=xq[:, tt, :].rearrange("p t c -> p (t c)").bitcast(FP8X4),
@@ -156,118 +167,152 @@ def tile_naivelstm_pa_kernel(
                 in_=xg[:, tt, :].rearrange("p t c -> p (t c)"),
             )
 
-        wh_tiles = {}
-        wq_tiles = {}
-
-        def prep_hidden_weights(k):
-            wh_t = whp.tile([P, 4, NG * P], F32, name="wh_t")
-            wh_tiles[k] = wh_t
-            for g in range(NG):
-                bank = transpose_words(raw_tiles[(1, k, g)][:].bitcast(F32))
-                copy(1, wh_t[:, :, g * P:(g + 1) * P], bank[:])
-                issue_load()
-
-        def hidden(k):
-            wv = wh_tiles[k][:].bitcast(BF16).rearrange("p j (c e) -> p j c e", e=2)
-            bank = psum.tile([P, NG * P], F32, name="hid", tag="bank")
-            for j in range(4):
-                for e in range(2):
-                    nc.tensor.matmul(
-                        bank[:], lhsT=h_t[:, j, e, :], rhs=wv[:, j, :, e],
-                        start=(j == 0 and e == 0), stop=False,
-                    )
-            nc.tensor.matmul(
-                bank[:], lhsT=ones[:],
-                rhs=bias_sb[:, k, :, :].rearrange("p g r -> p (g r)"),
-                start=False, stop=True,
-            )
-            copy(1, gsum[:, k, :], bank[:])
-
-        def prep_input_weights(k):
-            wg = wgp.tile([P, 2, NG, 4 * P], BF16, name="wg", align_bytes=64)
+        def quantise_w(k):
+            wg = wg_tiles[k]
             wq = wqp.tile([P, 2, NG * P], U32, name="wq", align_bytes=64)
             ws = wqp.tile([P, 2, NG * P], U8, name="ws", align_bytes=64)
             wq_tiles[k] = (wq, ws)
-            for g in range(NG):
-                bank = transpose_words(raw_tiles[(0, k, g)][:].bitcast(F32))
-                copy(
-                    0 if g < 2 else 1,
-                    wg[:].bitcast(F32)[:, :, g, :].rearrange("p g (r u) -> p g r u", u=2),
-                    regrouped(bank),
-                )
-                issue_load()
             nc.vector.quantize_mx(
                 out=wq[:].rearrange("p g c -> p (g c)").bitcast(FP8X4),
                 scales=ws[:].rearrange("p g c -> p (g c)"),
                 in_=wg[:].rearrange("p g n c -> p (g n c)"),
             )
 
-        def gates(k, tg):
-            wq, ws = wq_tiles[k]
-            z = zp.tile([P, NG, NT, P], F32, name="z")
-            for tl in range(NT):
-                t = tg * NT + tl
-                bank = psum.tile([P, NG, P], F32, name="mx", tag="bank")
-                for g in range(2):
-                    cols = slice(g * P, (g + 1) * P)
-                    nc.tensor.matmul_mx(
-                        out=bank[:].rearrange("p g r -> p (g r)"),
-                        lhsT=xq[:, t, cols].bitcast(FP8X4),
-                        lhsT_scale=xs[:, t, cols],
-                        rhs=wq[:, g, :].bitcast(FP8X4),
-                        rhs_scale=ws[:, g, :],
-                        start=(g == 0),
-                        stop=(g == 1),
-                    )
-                nc.vector.tensor_tensor(
-                    out=z[:, :, tl, :],
-                    in0=bank[:],
-                    in1=gsum[:, k, :].rearrange("p (g r) -> p g r", g=NG),
-                    op=ALU.add,
-                )
-            return z
+        def product(engine, out, in0, in1, op):
+            if engine == 0:
+                nc.vector.tensor_tensor(out=out, in0=in0, in1=in1, op=op)
+            else:
+                nc.gpsimd.tensor_tensor(out=out, in0=in0, in1=in1, op=op)
 
-        def elementwise(k, tg, z):
+        def finish(u):
+            k, half = divmod(u, 2)
             ks = slice(k * P, (k + 1) * P)
-            sig = z[:, 0:3, :, :].rearrange("p g t r -> p (g t r)")
-            nc.scalar.activation(out=sig, in_=sig, func=ACT.Sigmoid)
-            nc.scalar.activation(out=z[:, 3], in_=z[:, 3], func=ACT.Tanh)
-            nc.gpsimd.tensor_tensor(
-                out=z[:, 1], in0=z[:, 1],
-                in1=c0_sb[:, ks].unsqueeze(1).to_broadcast([P, NT, P]),
-                op=ALU.mult,
-            )
-            nc.gpsimd.tensor_tensor(out=z[:, 0], in0=z[:, 0], in1=z[:, 3], op=ALU.mult)
-            nc.vector.tensor_tensor(out=z[:, 3], in0=z[:, 0], in1=z[:, 1], op=ALU.add)
-            nc.scalar.activation(out=z[:, 1], in_=z[:, 3], func=ACT.Tanh)
+            z = z_tiles[u]
             hout = hp.tile([P, NT, P], F32, name="hout")
             nc.vector.tensor_tensor(out=hout[:], in0=z[:, 2], in1=z[:, 1], op=ALU.mult)
-            t0 = tg * NT
+            t0 = half * NT
             nc.sync.dma_start(
                 out=out_0[t0:t0 + NT, :, ks].rearrange("t b h -> b t h"), in_=hout[:]
             )
-            if t0 + NT == T:
+            if half == 1:
                 nc.sync.dma_start(out=out_1[0, :, ks], in_=hout[:, NT - 1, :])
                 nc.sync.dma_start(out=out_2[0, :, ks], in_=z[:, 3, NT - 1, :])
 
-        prep_h0()
-        prep_hidden_weights(0)
-        hidden(0)
-        prep_x(0)
-        prep_x(1)
-        prep_hidden_weights(1)
-        hidden(1)
-        prep_x(2)
-        prep_x(3)
-        prep_input_weights(0)
-        for k in range(NCH):
-            if k + 2 < NCH:
-                prep_hidden_weights(k + 2)
-            z = gates(k, 0)
-            elementwise(k, 0, z)
-            if k + 1 < NCH:
-                prep_input_weights(k + 1)
-            if k + 2 < NCH:
-                hidden(k + 2)
-            z = gates(k, 1)
-            elementwise(k, 1, z)
+        def elementwise(s):
+            a = s - 1
+            if 0 <= a < NU:
+                z = z_tiles[a]
+                k = a // 2
+                eng = 0 if a >= NU - TAIL_V else 1
+                sig = z[:, 0:3, :, :].rearrange("p g t r -> p (g t r)")
+                nc.scalar.activation(out=sig, in_=sig, func=ACT.Sigmoid)
+                product(
+                    eng, z[:, 1], z[:, 1],
+                    c0_sb[:, k * P:(k + 1) * P].unsqueeze(1).to_broadcast([P, NT, P]),
+                    ALU.mult,
+                )
+                nc.scalar.activation(out=z[:, 3], in_=z[:, 3], func=ACT.Tanh)
+                product(eng, z[:, 0], z[:, 0], z[:, 3], ALU.mult)
+                product(eng, z[:, 3], z[:, 0], z[:, 1], ALU.add)
+            b = s - 2
+            if 0 <= b < NU:
+                z = z_tiles[b]
+                nc.scalar.activation(out=z[:, 1], in_=z[:, 3], func=ACT.Tanh)
+                state["late"] = lambda: finish(b)
+
+        for kind, k in plan:
+            if kind == "h0":
+                bank = transpose_words(h0_raw[:].bitcast(F32))
+                nc.vector.tensor_copy(
+                    out=h_t[:],
+                    in_=bank[:].bitcast(BF16).rearrange("p j (b e) -> p j e b", e=2),
+                )
+            elif kind == "x":
+                banks = [
+                    transpose_words(x_raw[:].bitcast(F32)[:, t, :]) for t in (2 * k, 2 * k + 1)
+                ]
+                for n in range(2):
+                    copy(
+                        COPY_X[n],
+                        xg[:].bitcast(F32)[:, 2 * k + n, :].rearrange(
+                            "p (g r u) -> p g r u", g=2, u=2
+                        ),
+                        regrouped(banks[n]),
+                    )
+                flush_pending()
+                state["pending"].append(lambda pair=k: quantise_x(pair))
+            elif kind == "H":
+                wh_t = whp.tile([P, 4, NG * P], F32, name="wh_t")
+                wh_tiles[k] = wh_t
+                banks = []
+                for g in range(NG):
+                    banks.append(transpose_words(raw_tiles[("H", k, g)][:].bitcast(F32)))
+                    issue_load()
+                for g in range(NG):
+                    copy(COPY_H[g], wh_t[:, :, g * P:(g + 1) * P], banks[g][:])
+                flush_pending()
+                run_late()
+            elif kind == "I":
+                wg = wgp.tile([P, 2, NG, 4 * P], BF16, name="wg", align_bytes=64)
+                wg_tiles[k] = wg
+                banks = []
+                for g in range(NG):
+                    banks.append(transpose_words(raw_tiles[("I", k, g)][:].bitcast(F32)))
+                    issue_load()
+                for g in range(NG):
+                    copy(
+                        COPY_I[g],
+                        wg[:].bitcast(F32)[:, :, g, :].rearrange("p g (r u) -> p g r u", u=2),
+                        regrouped(banks[g]),
+                    )
+                flush_pending()
+                run_late()
+                state["pending"].append(lambda chunk=k: quantise_w(chunk))
+            elif kind == "hid":
+                wv = wh_tiles[k][:].bitcast(BF16).rearrange("p j (c e) -> p j c e", e=2)
+                bank = psum.tile([P, NG * P], F32, name="hid", tag="bank")
+                for j in range(4):
+                    for e in range(2):
+                        nc.tensor.matmul(
+                            bank[:], lhsT=h_t[:, j, e, :], rhs=wv[:, j, :, e],
+                            start=(j == 0 and e == 0), stop=False,
+                        )
+                nc.tensor.matmul(
+                    bank[:], lhsT=ones[:],
+                    rhs=bias_sb[:, k, :, :].rearrange("p g r -> p (g r)"),
+                    start=False, stop=True,
+                )
+                flush_pending()
+                copy(COPY_G, gsum[:, k, :], bank[:])
+            else:
+                flush_pending()
+                run_late()
+                chunk, half = divmod(k, 2)
+                wq, ws = wq_tiles[chunk]
+                z = zp.tile([P, NG, NT, P], F32, name="z")
+                z_tiles[k] = z
+                for tl in range(NT):
+                    t = half * NT + tl
+                    bank = psum.tile([P, NG, P], F32, name="mx", tag="bank")
+                    for g in range(2):
+                        cols = slice(g * P, (g + 1) * P)
+                        nc.tensor.matmul_mx(
+                            out=bank[:].rearrange("p g r -> p (g r)"),
+                            lhsT=xq[:, t, cols].bitcast(FP8X4),
+                            lhsT_scale=xs[:, t, cols],
+                            rhs=wq[:, g, :].bitcast(FP8X4),
+                            rhs_scale=ws[:, g, :],
+                            start=(g == 0),
+                            stop=(g == 1),
+                        )
+                    nc.vector.tensor_tensor(
+                        out=z[:, :, tl, :],
+                        in0=bank[:],
+                        in1=gsum[:, chunk, :].rearrange("p (g r) -> p g r", g=NG),
+                        op=ALU.add,
+                    )
+                elementwise(k)
+        run_late()
+        for s in range(NU, NU + 2):
+            elementwise(s)
+            run_late()

@@ -20,9 +20,10 @@ NT = 4
 RAW_BUFS = 24
 PINNED = True
 NU = 2 * NCH
-TAIL_V = 3
+TAIL_V = 2
+PRODUCTS = (0, 1, 1)
 COPY_X = (0, 1)
-COPY_I = (0, 0, 0, 1)
+COPY_I = (0, 0, 1, 1)
 COPY_H = (1, 1, 1, 1)
 COPY_G = 1
 
@@ -75,15 +76,14 @@ def tile_naivelstm_pa_kernel(
         nc.vector.memset(ones[:], 1.0)
         nc.vector.memset(bias_sb[:].bitcast(I32), 0)
 
-        plan = [("x", 0), ("x", 1), ("I", 0), ("h0", 0), ("H", 0), ("hid", 0)]
-        for u in range(NU):
+        plan = [
+            ("h0", 0), ("H", 0), ("x", 0), ("hid", 0), ("x", 1), ("I", 0),
+            ("x", 2), ("x", 3), ("H", 1), ("U", 0), ("U", 1), ("I", 1), ("hid", 1), ("H", 2),
+        ]
+        for u in range(2, NU):
             k, half = divmod(u, 2)
             plan.append(("U", u))
-            if u == 0:
-                plan.extend([("x", 2), ("x", 3), ("H", 1)])
-            elif u == 1:
-                plan.extend([("I", 1), ("hid", 1), ("H", 2)])
-            elif half == 0 and k + 1 < NCH:
+            if half == 0 and k + 1 < NCH:
                 plan.extend([("I", k + 1), ("hid", k + 1)])
             elif half == 1 and k + 2 < NCH:
                 plan.append(("H", k + 2))
@@ -203,17 +203,17 @@ def tile_naivelstm_pa_kernel(
             if 0 <= a < NU:
                 z = z_tiles[a]
                 k = a // 2
-                eng = 0 if a >= NU - TAIL_V else 1
+                eng = (0, 0, 0) if a >= NU - TAIL_V else PRODUCTS
                 sig = z[:, 0:3, :, :].rearrange("p g t r -> p (g t r)")
                 nc.scalar.activation(out=sig, in_=sig, func=ACT.Sigmoid)
                 product(
-                    eng, z[:, 1], z[:, 1],
+                    eng[0], z[:, 1], z[:, 1],
                     c0_sb[:, k * P:(k + 1) * P].unsqueeze(1).to_broadcast([P, NT, P]),
                     ALU.mult,
                 )
                 nc.scalar.activation(out=z[:, 3], in_=z[:, 3], func=ACT.Tanh)
-                product(eng, z[:, 0], z[:, 0], z[:, 3], ALU.mult)
-                product(eng, z[:, 3], z[:, 0], z[:, 1], ALU.add)
+                product(eng[1], z[:, 0], z[:, 0], z[:, 3], ALU.mult)
+                product(eng[2], z[:, 3], z[:, 0], z[:, 1], ALU.add)
             b = s - 2
             if 0 <= b < NU:
                 z = z_tiles[b]
@@ -249,7 +249,7 @@ def tile_naivelstm_pa_kernel(
                     banks.append(transpose_words(raw_tiles[("H", k, g)][:].bitcast(F32)))
                     issue_load()
                 for g in range(NG):
-                    copy(COPY_H[g], wh_t[:, :, g * P:(g + 1) * P], banks[g][:])
+                    copy((1, 0, 1, 0)[g] if k == 0 else COPY_H[g], wh_t[:, :, g * P:(g + 1) * P], banks[g][:])
                 flush_pending()
                 run_late()
             elif kind == "I":
@@ -261,7 +261,7 @@ def tile_naivelstm_pa_kernel(
                     issue_load()
                 for g in range(NG):
                     copy(
-                        COPY_I[g],
+                        (0, 1, 0, 1)[g] if k == 0 else COPY_I[g],
                         wg[:].bitcast(F32)[:, :, g, :].rearrange("p g (r u) -> p g r u", u=2),
                         regrouped(banks[g]),
                     )

@@ -17,15 +17,10 @@ B, T, I, H = 128, 8, 1024, 1024
 NG = 4
 NCH = H // P
 NT = 4
+NU = NCH * (T // NT)
+QUARTERS = 4
 RAW_BUFS = 24
-PINNED = True
-NU = 2 * NCH
-TAIL_V = 2
-PRODUCTS = (0, 1, 1)
-COPY_X = (0, 1)
-COPY_I = (0, 0, 1, 1)
-COPY_H = (1, 1, 1, 1)
-COPY_G = 1
+LAST_ON_VECTOR = 2
 
 FLOPS = 2 * B * T * I * NG * H + 2 * B * H * NG * H
 
@@ -45,9 +40,17 @@ def tile_naivelstm_pa_kernel(
     b_in = [b_ii, b_if_, b_io, b_ig]
     b_hid = [b_hi, b_hf, b_ho, b_hg]
 
+    by_vector = nc.vector.tensor_copy
+    by_scalar = nc.scalar.copy
+    on_vector = nc.vector.tensor_tensor
+    on_gpsimd = nc.gpsimd.tensor_tensor
+    copies_hidden = (by_scalar, by_scalar, by_scalar, by_scalar)
+    copies_input = (by_vector, by_scalar, by_scalar, by_scalar)
+    copies_hidden_first = (by_scalar, by_vector, by_scalar, by_vector)
+    copies_input_first = (by_vector, by_scalar, by_vector, by_scalar)
+
     with ExitStack() as ctx:
-        if PINNED:
-            ctx.enter_context(tc.manual_schedule())
+        ctx.enter_context(tc.manual_schedule())
         const = ctx.enter_context(tc.tile_pool(name="const", bufs=1))
         raw = ctx.enter_context(tc.tile_pool(name="raw", bufs=RAW_BUFS))
         wgp = ctx.enter_context(tc.tile_pool(name="wgp", bufs=2))
@@ -63,7 +66,7 @@ def tile_naivelstm_pa_kernel(
         bias_sb = const.tile([P, NCH, NG, P], BF16, name="bias_sb")
         h0_raw = const.tile([P, H], BF16, name="h0_raw")
         c0_sb = const.tile([P, H], BF16, name="c0_sb")
-        h_t = const.tile([P, 4, 2, P], BF16, name="h_t")
+        h_t = const.tile([P, QUARTERS, 2, P], BF16, name="h_t")
         x_raw = const.tile([P, T, I], BF16, name="x_raw")
         xg = const.tile([P, T, I], BF16, name="xg", align_bytes=64)
         xq = const.tile([P, T, I // 4], U32, name="xq", align_bytes=64)
@@ -76,118 +79,188 @@ def tile_naivelstm_pa_kernel(
         nc.vector.memset(ones[:], 1.0)
         nc.vector.memset(bias_sb[:].bitcast(I32), 0)
 
-        plan = [
-            ("h0", 0), ("H", 0), ("x", 0), ("hid", 0), ("x", 1), ("I", 0),
-            ("x", 2), ("x", 3), ("H", 1), ("U", 0), ("U", 1), ("I", 1), ("hid", 1), ("H", 2),
-        ]
-        for u in range(2, NU):
-            k, half = divmod(u, 2)
-            plan.append(("U", u))
-            if half == 0 and k + 1 < NCH:
-                plan.extend([("I", k + 1), ("hid", k + 1)])
-            elif half == 1 and k + 2 < NCH:
-                plan.append(("H", k + 2))
-
-        blocks = []
-        for kind, k in plan:
-            if kind == "H" or kind == "I":
-                blocks.extend([(kind, k, g) for g in range(NG)])
+        blocks = [(kind, k, gate) for k in range(NCH) for kind in ("H", "I") for gate in range(NG)]
         raw_tiles = {}
-        cursor = [0]
+        loaded = [0]
 
-        def issue_load():
-            n = cursor[0]
-            if n < len(blocks):
-                kind, k, g = blocks[n]
-                w = w_hid[g] if kind == "H" else w_in[g]
+        def load_next_block():
+            index = loaded[0]
+            if index < len(blocks):
+                kind, k, gate = blocks[index]
+                w = w_hid[gate] if kind == "H" else w_in[gate]
                 wraw = raw.tile([P, I], BF16, name="wraw", tag="wraw")
                 nc.sync.dma_start(out=wraw[:], in_=w[k * P:(k + 1) * P, :])
-                raw_tiles[blocks[n]] = wraw
-                cursor[0] = n + 1
+                raw_tiles[blocks[index]] = wraw
+                loaded[0] = index + 1
 
-        for kind, k in plan:
-            if kind == "h0":
-                nc.sync.dma_start(out=h0_raw[:], in_=h0[0])
-            elif kind == "x":
-                nc.sync.dma_start(
-                    out=x_raw[:, 2 * k:2 * k + 2, :], in_=inputs[:, 2 * k:2 * k + 2, :]
-                )
-            elif (kind == "H" or kind == "I") and cursor[0] < RAW_BUFS:
-                for g in range(NG):
-                    issue_load()
-        for g in range(NG):
+        def load_x(pair):
+            steps = slice(2 * pair, 2 * pair + 2)
+            nc.sync.dma_start(out=x_raw[:, steps, :], in_=inputs[:, steps, :])
+
+        nc.sync.dma_start(out=h0_raw[:], in_=h0[0])
+        for gate in range(NG):
+            load_next_block()
+        load_x(0)
+        load_x(1)
+        for gate in range(NG):
+            load_next_block()
+        load_x(2)
+        load_x(3)
+        for count in range(RAW_BUFS - 2 * NG):
+            load_next_block()
+        for gate in range(NG):
             nc.scalar.dma_start(
-                out=bias_sb[0:1, :, g, :],
-                in_=b_in[g].rearrange("(k r) o -> o k r", r=P),
+                out=bias_sb[0:1, :, gate, :],
+                in_=b_in[gate].rearrange("(k r) o -> o k r", r=P),
             )
             nc.scalar.dma_start(
-                out=bias_sb[1:2, :, g, :],
-                in_=b_hid[g].rearrange("(k r) o -> o k r", r=P),
+                out=bias_sb[1:2, :, gate, :],
+                in_=b_hid[gate].rearrange("(k r) o -> o k r", r=P),
             )
         nc.scalar.dma_start(out=c0_sb[:], in_=c0[0])
 
-        def copy(engine, out, in_):
-            if engine == 0:
-                nc.vector.tensor_copy(out=out, in_=in_)
-            else:
-                nc.scalar.copy(out=out, in_=in_)
-
         def transpose_words(words):
-            bank = psum.tile([P, 4, P], F32, name="tp", tag="bank")
-            for q in range(4):
+            bank = psum.tile([P, QUARTERS, P], F32, name="tp", tag="bank")
+            for q in range(QUARTERS):
                 nc.tensor.transpose(bank[:, q, :], words[:, q * P:(q + 1) * P], ident[:])
             return bank
 
         def regrouped(bank):
             return bank[:].rearrange("p (g u) r -> p g r u", u=2)
 
+        def prepare_h0():
+            bank = transpose_words(h0_raw[:].bitcast(F32))
+            nc.vector.tensor_copy(
+                out=h_t[:],
+                in_=bank[:].bitcast(BF16).rearrange("p q (b e) -> p q e b", e=2),
+            )
+
+        def prepare_x(pair):
+            banks = [
+                transpose_words(x_raw[:].bitcast(F32)[:, t, :]) for t in (2 * pair, 2 * pair + 1)
+            ]
+            for odd, copy_out in enumerate((by_vector, by_scalar)):
+                copy_out(
+                    out=xg[:].bitcast(F32)[:, 2 * pair + odd, :].rearrange(
+                        "p (g r u) -> p g r u", g=2, u=2
+                    ),
+                    in_=regrouped(banks[odd]),
+                )
+
+        def quantise_x(pair):
+            steps = slice(2 * pair, 2 * pair + 2)
+            nc.vector.quantize_mx(
+                out=xq[:, steps, :].rearrange("p t c -> p (t c)").bitcast(FP8X4),
+                scales=xs[:, steps, :].rearrange("p t c -> p (t c)"),
+                in_=xg[:, steps, :].rearrange("p t c -> p (t c)"),
+            )
+
         wh_tiles = {}
         wg_tiles = {}
         wq_tiles = {}
         z_tiles = {}
-        state = {"late": None, "pending": []}
 
-        def flush_pending():
-            todo = state["pending"]
-            state["pending"] = []
-            for f in todo:
-                f()
+        def transpose_hidden_weights(k, copies):
+            wh_t = whp.tile([P, QUARTERS, NG * P], F32, name="wh_t")
+            wh_tiles[k] = wh_t
+            banks = []
+            for gate in range(NG):
+                banks.append(transpose_words(raw_tiles[("H", k, gate)][:].bitcast(F32)))
+                load_next_block()
+            for gate in range(NG):
+                copies[gate](out=wh_t[:, :, gate * P:(gate + 1) * P], in_=banks[gate][:])
 
-        def run_late():
-            f = state["late"]
-            state["late"] = None
-            if f is not None:
-                f()
-
-        def quantise_x(pair):
-            tt = slice(2 * pair, 2 * pair + 2)
-            nc.vector.quantize_mx(
-                out=xq[:, tt, :].rearrange("p t c -> p (t c)").bitcast(FP8X4),
-                scales=xs[:, tt, :].rearrange("p t c -> p (t c)"),
-                in_=xg[:, tt, :].rearrange("p t c -> p (t c)"),
+        def hidden_matmuls(k):
+            wv = wh_tiles[k][:].bitcast(BF16).rearrange("p q (c e) -> p q c e", e=2)
+            bank = psum.tile([P, NG * P], F32, name="hid", tag="bank")
+            for q in range(QUARTERS):
+                for e in range(2):
+                    nc.tensor.matmul(
+                        bank[:], lhsT=h_t[:, q, e, :], rhs=wv[:, q, :, e],
+                        start=(q == 0 and e == 0), stop=False,
+                    )
+            nc.tensor.matmul(
+                bank[:], lhsT=ones[:],
+                rhs=bias_sb[:, k, :, :].rearrange("p n r -> p (n r)"),
+                start=False, stop=True,
             )
+            return bank
 
-        def quantise_w(k):
-            wg = wg_tiles[k]
+        def keep_hidden_sum(k, bank):
+            by_scalar(out=gsum[:, k, :], in_=bank[:])
+
+        def transpose_input_weights(k, copies):
+            wg = wgp.tile([P, 2, NG, 4 * P], BF16, name="wg", align_bytes=64)
+            wg_tiles[k] = wg
+            banks = []
+            for gate in range(NG):
+                banks.append(transpose_words(raw_tiles[("I", k, gate)][:].bitcast(F32)))
+                load_next_block()
+            for gate in range(NG):
+                copies[gate](
+                    out=wg[:].bitcast(F32)[:, :, gate, :].rearrange("p g (r u) -> p g r u", u=2),
+                    in_=regrouped(banks[gate]),
+                )
+
+        def quantise_input_weights(k):
             wq = wqp.tile([P, 2, NG * P], U32, name="wq", align_bytes=64)
             ws = wqp.tile([P, 2, NG * P], U8, name="ws", align_bytes=64)
             wq_tiles[k] = (wq, ws)
             nc.vector.quantize_mx(
                 out=wq[:].rearrange("p g c -> p (g c)").bitcast(FP8X4),
                 scales=ws[:].rearrange("p g c -> p (g c)"),
-                in_=wg[:].rearrange("p g n c -> p (g n c)"),
+                in_=wg_tiles[k][:].rearrange("p g n c -> p (g n c)"),
             )
 
-        def product(engine, out, in0, in1, op):
-            if engine == 0:
-                nc.vector.tensor_tensor(out=out, in0=in0, in1=in1, op=op)
-            else:
-                nc.gpsimd.tensor_tensor(out=out, in0=in0, in1=in1, op=op)
+        def gate_sums(unit):
+            k, half = divmod(unit, 2)
+            wq, ws = wq_tiles[k]
+            z = zp.tile([P, NG, NT, P], F32, name="z")
+            z_tiles[unit] = z
+            for tl in range(NT):
+                t = half * NT + tl
+                bank = psum.tile([P, NG, P], F32, name="mx", tag="bank")
+                for g in range(2):
+                    cols = slice(g * P, (g + 1) * P)
+                    nc.tensor.matmul_mx(
+                        out=bank[:].rearrange("p n r -> p (n r)"),
+                        lhsT=xq[:, t, cols].bitcast(FP8X4),
+                        lhsT_scale=xs[:, t, cols],
+                        rhs=wq[:, g, :].bitcast(FP8X4),
+                        rhs_scale=ws[:, g, :],
+                        start=(g == 0),
+                        stop=(g == 1),
+                    )
+                nc.vector.tensor_tensor(
+                    out=z[:, :, tl, :],
+                    in0=bank[:],
+                    in1=gsum[:, k, :].rearrange("p (n r) -> p n r", n=NG),
+                    op=ALU.add,
+                )
 
-        def finish(u):
-            k, half = divmod(u, 2)
+        def gates(unit):
+            z = z_tiles[unit]
+            k = unit // 2
+            rest = on_vector if unit >= NU - LAST_ON_VECTOR else on_gpsimd
+            sig = z[:, 0:3, :, :].rearrange("p n t r -> p (n t r)")
+            nc.scalar.activation(out=sig, in_=sig, func=ACT.Sigmoid)
+            on_vector(
+                out=z[:, 1], in0=z[:, 1],
+                in1=c0_sb[:, k * P:(k + 1) * P].unsqueeze(1).to_broadcast([P, NT, P]),
+                op=ALU.mult,
+            )
+            nc.scalar.activation(out=z[:, 3], in_=z[:, 3], func=ACT.Tanh)
+            rest(out=z[:, 0], in0=z[:, 0], in1=z[:, 3], op=ALU.mult)
+            rest(out=z[:, 3], in0=z[:, 0], in1=z[:, 1], op=ALU.add)
+
+        def tanh_c(unit):
+            z = z_tiles[unit]
+            nc.scalar.activation(out=z[:, 1], in_=z[:, 3], func=ACT.Tanh)
+
+        def finish(unit):
+            k, half = divmod(unit, 2)
             ks = slice(k * P, (k + 1) * P)
-            z = z_tiles[u]
+            z = z_tiles[unit]
             hout = hp.tile([P, NT, P], F32, name="hout")
             nc.vector.tensor_tensor(out=hout[:], in0=z[:, 2], in1=z[:, 1], op=ALU.mult)
             t0 = half * NT
@@ -198,121 +271,43 @@ def tile_naivelstm_pa_kernel(
                 nc.sync.dma_start(out=out_1[0, :, ks], in_=hout[:, NT - 1, :])
                 nc.sync.dma_start(out=out_2[0, :, ks], in_=z[:, 3, NT - 1, :])
 
-        def elementwise(s):
-            a = s - 1
-            if 0 <= a < NU:
-                z = z_tiles[a]
-                k = a // 2
-                eng = (0, 0, 0) if a >= NU - TAIL_V else PRODUCTS
-                sig = z[:, 0:3, :, :].rearrange("p g t r -> p (g t r)")
-                nc.scalar.activation(out=sig, in_=sig, func=ACT.Sigmoid)
-                product(
-                    eng[0], z[:, 1], z[:, 1],
-                    c0_sb[:, k * P:(k + 1) * P].unsqueeze(1).to_broadcast([P, NT, P]),
-                    ALU.mult,
-                )
-                nc.scalar.activation(out=z[:, 3], in_=z[:, 3], func=ACT.Tanh)
-                product(eng[1], z[:, 0], z[:, 0], z[:, 3], ALU.mult)
-                product(eng[2], z[:, 3], z[:, 0], z[:, 1], ALU.add)
-            b = s - 2
-            if 0 <= b < NU:
-                z = z_tiles[b]
-                nc.scalar.activation(out=z[:, 1], in_=z[:, 3], func=ACT.Tanh)
-                state["late"] = lambda: finish(b)
+        prepare_h0()
+        transpose_hidden_weights(0, copies_hidden_first)
+        prepare_x(0)
+        bank = hidden_matmuls(0)
+        quantise_x(0)
+        keep_hidden_sum(0, bank)
+        prepare_x(1)
+        transpose_input_weights(0, copies_input_first)
+        quantise_x(1)
+        prepare_x(2)
+        quantise_input_weights(0)
+        prepare_x(3)
+        quantise_x(2)
+        transpose_hidden_weights(1, copies_hidden)
+        quantise_x(3)
+        gate_sums(0)
+        gate_sums(1)
+        gates(0)
+        transpose_input_weights(1, copies_input)
+        bank = hidden_matmuls(1)
+        quantise_input_weights(1)
+        keep_hidden_sum(1, bank)
+        transpose_hidden_weights(2, copies_hidden)
 
-        for kind, k in plan:
-            if kind == "h0":
-                bank = transpose_words(h0_raw[:].bitcast(F32))
-                nc.vector.tensor_copy(
-                    out=h_t[:],
-                    in_=bank[:].bitcast(BF16).rearrange("p j (b e) -> p j e b", e=2),
-                )
-            elif kind == "x":
-                banks = [
-                    transpose_words(x_raw[:].bitcast(F32)[:, t, :]) for t in (2 * k, 2 * k + 1)
-                ]
-                for n in range(2):
-                    copy(
-                        COPY_X[n],
-                        xg[:].bitcast(F32)[:, 2 * k + n, :].rearrange(
-                            "p (g r u) -> p g r u", g=2, u=2
-                        ),
-                        regrouped(banks[n]),
-                    )
-                flush_pending()
-                state["pending"].append(lambda pair=k: quantise_x(pair))
-            elif kind == "H":
-                wh_t = whp.tile([P, 4, NG * P], F32, name="wh_t")
-                wh_tiles[k] = wh_t
-                banks = []
-                for g in range(NG):
-                    banks.append(transpose_words(raw_tiles[("H", k, g)][:].bitcast(F32)))
-                    issue_load()
-                for g in range(NG):
-                    copy((1, 0, 1, 0)[g] if k == 0 else COPY_H[g], wh_t[:, :, g * P:(g + 1) * P], banks[g][:])
-                flush_pending()
-                run_late()
-            elif kind == "I":
-                wg = wgp.tile([P, 2, NG, 4 * P], BF16, name="wg", align_bytes=64)
-                wg_tiles[k] = wg
-                banks = []
-                for g in range(NG):
-                    banks.append(transpose_words(raw_tiles[("I", k, g)][:].bitcast(F32)))
-                    issue_load()
-                for g in range(NG):
-                    copy(
-                        (0, 1, 0, 1)[g] if k == 0 else COPY_I[g],
-                        wg[:].bitcast(F32)[:, :, g, :].rearrange("p g (r u) -> p g r u", u=2),
-                        regrouped(banks[g]),
-                    )
-                flush_pending()
-                run_late()
-                state["pending"].append(lambda chunk=k: quantise_w(chunk))
-            elif kind == "hid":
-                wv = wh_tiles[k][:].bitcast(BF16).rearrange("p j (c e) -> p j c e", e=2)
-                bank = psum.tile([P, NG * P], F32, name="hid", tag="bank")
-                for j in range(4):
-                    for e in range(2):
-                        nc.tensor.matmul(
-                            bank[:], lhsT=h_t[:, j, e, :], rhs=wv[:, j, :, e],
-                            start=(j == 0 and e == 0), stop=False,
-                        )
-                nc.tensor.matmul(
-                    bank[:], lhsT=ones[:],
-                    rhs=bias_sb[:, k, :, :].rearrange("p g r -> p (g r)"),
-                    start=False, stop=True,
-                )
-                flush_pending()
-                copy(COPY_G, gsum[:, k, :], bank[:])
-            else:
-                flush_pending()
-                run_late()
-                chunk, half = divmod(k, 2)
-                wq, ws = wq_tiles[chunk]
-                z = zp.tile([P, NG, NT, P], F32, name="z")
-                z_tiles[k] = z
-                for tl in range(NT):
-                    t = half * NT + tl
-                    bank = psum.tile([P, NG, P], F32, name="mx", tag="bank")
-                    for g in range(2):
-                        cols = slice(g * P, (g + 1) * P)
-                        nc.tensor.matmul_mx(
-                            out=bank[:].rearrange("p g r -> p (g r)"),
-                            lhsT=xq[:, t, cols].bitcast(FP8X4),
-                            lhsT_scale=xs[:, t, cols],
-                            rhs=wq[:, g, :].bitcast(FP8X4),
-                            rhs_scale=ws[:, g, :],
-                            start=(g == 0),
-                            stop=(g == 1),
-                        )
-                    nc.vector.tensor_tensor(
-                        out=z[:, :, tl, :],
-                        in0=bank[:],
-                        in1=gsum[:, chunk, :].rearrange("p (g r) -> p g r", g=NG),
-                        op=ALU.add,
-                    )
-                elementwise(k)
-        run_late()
-        for s in range(NU, NU + 2):
-            elementwise(s)
-            run_late()
+        for s in range(2, NU + 2):
+            k, half = divmod(s, 2)
+            if s < NU:
+                gate_sums(s)
+            if s - 1 < NU:
+                gates(s - 1)
+            tanh_c(s - 2)
+            if half == 0 and k + 1 < NCH:
+                transpose_input_weights(k + 1, copies_input)
+            elif half == 1 and k + 2 < NCH:
+                transpose_hidden_weights(k + 2, copies_hidden)
+            finish(s - 2)
+            if half == 0 and k + 1 < NCH:
+                bank = hidden_matmuls(k + 1)
+                quantise_input_weights(k + 1)
+                keep_hidden_sum(k + 1, bank)

from contextlib import ExitStack

import concourse.mybir as mybir
from concourse.masks import make_identity

F32 = mybir.dt.float32
BF16 = mybir.dt.bfloat16
U32 = mybir.dt.uint32
U8 = mybir.dt.uint8
I32 = mybir.dt.int32
FP8X4 = mybir.dt.float8_e4m3fn_x4
ACT = mybir.ActivationFunctionType
ALU = mybir.AluOpType

P = 128
B, T, I, H = 128, 8, 1024, 1024
NG = 4
NCH = H // P
NT = 4
NU = NCH * (T // NT)
QUARTERS = 4
RAW_BUFS = 24
LAST_ON_VECTOR = 2

FLOPS = 2 * B * T * I * NG * H + 2 * B * H * NG * H


def tile_naivelstm_pa_kernel(
    tc,
    inputs, h0, c0,
    w_ii, b_ii, w_hi, b_hi,
    w_if_, b_if_, w_hf, b_hf,
    w_io, b_io, w_ho, b_ho,
    w_ig, b_ig, w_hg, b_hg,
    out_0, out_1, out_2,
):
    nc = tc.nc
    w_in = [w_ii, w_if_, w_io, w_ig]
    w_hid = [w_hi, w_hf, w_ho, w_hg]
    b_in = [b_ii, b_if_, b_io, b_ig]
    b_hid = [b_hi, b_hf, b_ho, b_hg]

    by_vector = nc.vector.tensor_copy
    by_scalar = nc.scalar.copy
    on_vector = nc.vector.tensor_tensor
    on_gpsimd = nc.gpsimd.tensor_tensor
    copies_hidden = (by_scalar, by_scalar, by_scalar, by_scalar)
    copies_input = (by_vector, by_scalar, by_scalar, by_scalar)
    copies_hidden_first = (by_scalar, by_vector, by_scalar, by_vector)
    copies_input_first = (by_vector, by_scalar, by_vector, by_scalar)

    with ExitStack() as ctx:
        ctx.enter_context(tc.manual_schedule())
        const = ctx.enter_context(tc.tile_pool(name="const", bufs=1))
        raw = ctx.enter_context(tc.tile_pool(name="raw", bufs=RAW_BUFS))
        wgp = ctx.enter_context(tc.tile_pool(name="wgp", bufs=2))
        wqp = ctx.enter_context(tc.tile_pool(name="wqp", bufs=3))
        whp = ctx.enter_context(tc.tile_pool(name="whp", bufs=2))
        zp = ctx.enter_context(tc.tile_pool(name="zp", bufs=4))
        hp = ctx.enter_context(tc.tile_pool(name="hp", bufs=3))
        psum = ctx.enter_context(tc.psum_pool(name="psum", bufs=8))

        ident = const.tile([P, P], F32, name="ident")
        ones = const.tile([P, P], BF16, name="ones")
        scratch = const.tile([P, 1], F32, name="scratch")
        bias_sb = const.tile([P, NCH, NG, P], BF16, name="bias_sb")
        h0_raw = const.tile([P, H], BF16, name="h0_raw")
        c0_sb = const.tile([P, H], BF16, name="c0_sb")
        h_t = const.tile([P, QUARTERS, 2, P], BF16, name="h_t")
        x_raw = const.tile([P, T, I], BF16, name="x_raw")
        xg = const.tile([P, T, I], BF16, name="xg", align_bytes=64)
        xq = const.tile([P, T, I // 4], U32, name="xq", align_bytes=64)
        xs = const.tile([P, T, I // 4], U8, name="xs", align_bytes=64)
        gsum = const.tile([P, NCH, NG * P], F32, name="gsum")

        make_identity(nc, ident[:])
        nc.vector.memset(scratch[:], 0.0)
        nc.scalar.activation(out=scratch[:], in_=scratch[:], func=ACT.Sigmoid)
        nc.vector.memset(ones[:], 1.0)
        nc.vector.memset(bias_sb[:].bitcast(I32), 0)

        blocks = [(kind, k, gate) for k in range(NCH) for kind in ("H", "I") for gate in range(NG)]
        raw_tiles = {}
        loaded = [0]

        def load_next_block():
            index = loaded[0]
            if index < len(blocks):
                kind, k, gate = blocks[index]
                w = w_hid[gate] if kind == "H" else w_in[gate]
                wraw = raw.tile([P, I], BF16, name="wraw", tag="wraw")
                nc.sync.dma_start(out=wraw[:], in_=w[k * P:(k + 1) * P, :])
                raw_tiles[blocks[index]] = wraw
                loaded[0] = index + 1

        def load_x(pair):
            steps = slice(2 * pair, 2 * pair + 2)
            nc.sync.dma_start(out=x_raw[:, steps, :], in_=inputs[:, steps, :])

        nc.sync.dma_start(out=h0_raw[:], in_=h0[0])
        for gate in range(NG):
            load_next_block()
        load_x(0)
        load_x(1)
        for gate in range(NG):
            load_next_block()
        load_x(2)
        load_x(3)
        for count in range(RAW_BUFS - 2 * NG):
            load_next_block()
        for gate in range(NG):
            nc.scalar.dma_start(
                out=bias_sb[0:1, :, gate, :],
                in_=b_in[gate].rearrange("(k r) o -> o k r", r=P),
            )
            nc.scalar.dma_start(
                out=bias_sb[1:2, :, gate, :],
                in_=b_hid[gate].rearrange("(k r) o -> o k r", r=P),
            )
        nc.scalar.dma_start(out=c0_sb[:], in_=c0[0])

        def transpose_words(words):
            bank = psum.tile([P, QUARTERS, P], F32, name="tp", tag="bank")
            for q in range(QUARTERS):
                nc.tensor.transpose(bank[:, q, :], words[:, q * P:(q + 1) * P], ident[:])
            return bank

        def regrouped(bank):
            return bank[:].rearrange("p (g u) r -> p g r u", u=2)

        def prepare_h0():
            bank = transpose_words(h0_raw[:].bitcast(F32))
            nc.vector.tensor_copy(
                out=h_t[:],
                in_=bank[:].bitcast(BF16).rearrange("p q (b e) -> p q e b", e=2),
            )

        def prepare_x(pair):
            banks = [
                transpose_words(x_raw[:].bitcast(F32)[:, t, :]) for t in (2 * pair, 2 * pair + 1)
            ]
            for odd, copy_out in enumerate((by_vector, by_scalar)):
                copy_out(
                    out=xg[:].bitcast(F32)[:, 2 * pair + odd, :].rearrange(
                        "p (g r u) -> p g r u", g=2, u=2
                    ),
                    in_=regrouped(banks[odd]),
                )

        def quantise_x(pair):
            steps = slice(2 * pair, 2 * pair + 2)
            nc.vector.quantize_mx(
                out=xq[:, steps, :].rearrange("p t c -> p (t c)").bitcast(FP8X4),
                scales=xs[:, steps, :].rearrange("p t c -> p (t c)"),
                in_=xg[:, steps, :].rearrange("p t c -> p (t c)"),
            )

        wh_tiles = {}
        wg_tiles = {}
        wq_tiles = {}
        z_tiles = {}

        def transpose_hidden_weights(k, copies):
            wh_t = whp.tile([P, QUARTERS, NG * P], F32, name="wh_t")
            wh_tiles[k] = wh_t
            banks = []
            for gate in range(NG):
                banks.append(transpose_words(raw_tiles[("H", k, gate)][:].bitcast(F32)))
                load_next_block()
            for gate in range(NG):
                copies[gate](out=wh_t[:, :, gate * P:(gate + 1) * P], in_=banks[gate][:])

        def hidden_matmuls(k):
            wv = wh_tiles[k][:].bitcast(BF16).rearrange("p q (c e) -> p q c e", e=2)
            bank = psum.tile([P, NG * P], F32, name="hid", tag="bank")
            for q in range(QUARTERS):
                for e in range(2):
                    nc.tensor.matmul(
                        bank[:], lhsT=h_t[:, q, e, :], rhs=wv[:, q, :, e],
                        start=(q == 0 and e == 0), stop=False,
                    )
            nc.tensor.matmul(
                bank[:], lhsT=ones[:],
                rhs=bias_sb[:, k, :, :].rearrange("p n r -> p (n r)"),
                start=False, stop=True,
            )
            return bank

        def keep_hidden_sum(k, bank):
            by_scalar(out=gsum[:, k, :], in_=bank[:])

        def transpose_input_weights(k, copies):
            wg = wgp.tile([P, 2, NG, 4 * P], BF16, name="wg", align_bytes=64)
            wg_tiles[k] = wg
            banks = []
            for gate in range(NG):
                banks.append(transpose_words(raw_tiles[("I", k, gate)][:].bitcast(F32)))
                load_next_block()
            for gate in range(NG):
                copies[gate](
                    out=wg[:].bitcast(F32)[:, :, gate, :].rearrange("p g (r u) -> p g r u", u=2),
                    in_=regrouped(banks[gate]),
                )

        def quantise_input_weights(k):
            wq = wqp.tile([P, 2, NG * P], U32, name="wq", align_bytes=64)
            ws = wqp.tile([P, 2, NG * P], U8, name="ws", align_bytes=64)
            wq_tiles[k] = (wq, ws)
            nc.vector.quantize_mx(
                out=wq[:].rearrange("p g c -> p (g c)").bitcast(FP8X4),
                scales=ws[:].rearrange("p g c -> p (g c)"),
                in_=wg_tiles[k][:].rearrange("p g n c -> p (g n c)"),
            )

        def gate_sums(unit):
            k, half = divmod(unit, 2)
            wq, ws = wq_tiles[k]
            z = zp.tile([P, NG, NT, P], F32, name="z")
            z_tiles[unit] = z
            for tl in range(NT):
                t = half * NT + tl
                bank = psum.tile([P, NG, P], F32, name="mx", tag="bank")
                for g in range(2):
                    cols = slice(g * P, (g + 1) * P)
                    nc.tensor.matmul_mx(
                        out=bank[:].rearrange("p n r -> p (n r)"),
                        lhsT=xq[:, t, cols].bitcast(FP8X4),
                        lhsT_scale=xs[:, t, cols],
                        rhs=wq[:, g, :].bitcast(FP8X4),
                        rhs_scale=ws[:, g, :],
                        start=(g == 0),
                        stop=(g == 1),
                    )
                nc.vector.tensor_tensor(
                    out=z[:, :, tl, :],
                    in0=bank[:],
                    in1=gsum[:, k, :].rearrange("p (n r) -> p n r", n=NG),
                    op=ALU.add,
                )

        def gates(unit):
            z = z_tiles[unit]
            k = unit // 2
            rest = on_vector if unit >= NU - LAST_ON_VECTOR else on_gpsimd
            sig = z[:, 0:3, :, :].rearrange("p n t r -> p (n t r)")
            nc.scalar.activation(out=sig, in_=sig, func=ACT.Sigmoid)
            on_vector(
                out=z[:, 1], in0=z[:, 1],
                in1=c0_sb[:, k * P:(k + 1) * P].unsqueeze(1).to_broadcast([P, NT, P]),
                op=ALU.mult,
            )
            nc.scalar.activation(out=z[:, 3], in_=z[:, 3], func=ACT.Tanh)
            rest(out=z[:, 0], in0=z[:, 0], in1=z[:, 3], op=ALU.mult)
            rest(out=z[:, 3], in0=z[:, 0], in1=z[:, 1], op=ALU.add)

        def tanh_c(unit):
            z = z_tiles[unit]
            nc.scalar.activation(out=z[:, 1], in_=z[:, 3], func=ACT.Tanh)

        def finish(unit):
            k, half = divmod(unit, 2)
            ks = slice(k * P, (k + 1) * P)
            z = z_tiles[unit]
            hout = hp.tile([P, NT, P], F32, name="hout")
            nc.vector.tensor_tensor(out=hout[:], in0=z[:, 2], in1=z[:, 1], op=ALU.mult)
            t0 = half * NT
            nc.sync.dma_start(
                out=out_0[t0:t0 + NT, :, ks].rearrange("t b h -> b t h"), in_=hout[:]
            )
            if half == 1:
                nc.sync.dma_start(out=out_1[0, :, ks], in_=hout[:, NT - 1, :])
                nc.sync.dma_start(out=out_2[0, :, ks], in_=z[:, 3, NT - 1, :])

        prepare_h0()
        transpose_hidden_weights(0, copies_hidden_first)
        prepare_x(0)
        bank = hidden_matmuls(0)
        quantise_x(0)
        keep_hidden_sum(0, bank)
        prepare_x(1)
        transpose_input_weights(0, copies_input_first)
        quantise_x(1)
        prepare_x(2)
        quantise_input_weights(0)
        prepare_x(3)
        quantise_x(2)
        transpose_hidden_weights(1, copies_hidden)
        quantise_x(3)
        gate_sums(0)
        gate_sums(1)
        gates(0)
        transpose_input_weights(1, copies_input)
        bank = hidden_matmuls(1)
        quantise_input_weights(1)
        keep_hidden_sum(1, bank)
        transpose_hidden_weights(2, copies_hidden)

        for s in range(2, NU + 2):
            k, half = divmod(s, 2)
            if s < NU:
                gate_sums(s)
            if s - 1 < NU:
                gates(s - 1)
            tanh_c(s - 2)
            if half == 0 and k + 1 < NCH:
                transpose_input_weights(k + 1, copies_input)
            elif half == 1 and k + 2 < NCH:
                transpose_hidden_weights(k + 2, copies_hidden)
            finish(s - 2)
            if half == 0 and k + 1 < NCH:
                bank = hidden_matmuls(k + 1)
                quantise_input_weights(k + 1)
                keep_hidden_sum(k + 1, bank)
